import numpy as np
import ml_dtypes


def mxq(x, axis, fmt="e4m3"):
    dtype, down = {"e4m3": (ml_dtypes.float8_e4m3fn, 7), "e5m2": (ml_dtypes.float8_e5m2, 14)}[fmt]
    v = np.moveaxis(np.asarray(x, np.float32).astype(ml_dtypes.bfloat16).astype(np.float64), axis, -1)
    blocks = v.reshape(v.shape[:-1] + (-1, 32))
    amax = np.abs(blocks).max(-1, keepdims=True)
    byte = np.maximum(np.where(amax > 0, np.frexp(amax)[1] - 1 + 127, 0) - down, 1)
    scale = np.exp2(byte - 127.0)
    codes = (blocks / scale).astype(np.float32).astype(dtype).astype(np.float64)
    return np.moveaxis((codes * scale).reshape(v.shape), -1, axis)


WIDE = False


def mx_kscale(k):
    if not WIDE:
        return np.ones(k)
    levels = np.array([10, -10, 5, -5, 0])
    if k % 512:
        return np.exp2(np.random.permutation(np.resize(levels, k // 32))).repeat(32)
    a = np.empty((k // 512, 16))
    for p in range(k // 512):
        a[p, :8] = np.random.permutation(np.resize(levels, 8))
        for g in range(8):
            far = levels[np.abs(levels - a[p, g]) >= 10]
            a[p, g + 8] = far[np.random.randint(len(far))]
    return np.exp2(a.ravel()).repeat(32)


BF16 = ml_dtypes.bfloat16


def bf(x):
    return np.asarray(x, np.float32).astype(BF16)


def f64(x):
    return np.asarray(x).astype(np.float64)


B, S, D, H, DH = 2, 256, 2048, 16, 128
E = H * DH
EPS = 1e-6
MU = 0.5


def setup_inputs():
    s = mx_kscale(D)
    g = np.random.standard_normal((D, H, DH))
    g = (g - g.mean(-1, keepdims=True)) / np.sqrt(D * (1.0 + MU * MU))
    lev = 2.5 + np.random.random((1, H, 1))
    w = (g + lev / (D * MU * DH)).reshape(D, E)
    x = np.random.standard_normal((B, S, D)) + MU
    return {"x": bf(x * s), "w": bf(w / s[:, None])}


def reference(x, w):
    y = mxq(f64(x), 2, "e4m3") @ mxq(f64(w), 0, "e4m3")
    yh = y.reshape(B, S, H, DH).transpose(0, 2, 1, 3)
    return yh / (yh.sum(-1, keepdims=True) + EPS)

@@ -1,0 +1,190 @@
+from contextlib import ExitStack
+
+import concourse.mybir as mybir
+from concourse.masks import make_identity
+
+F32 = mybir.dt.float32
+BF16 = mybir.dt.bfloat16
+U32 = mybir.dt.uint32
+U8 = mybir.dt.uint8
+FP8X4 = mybir.dt.float8_e4m3fn_x4
+COPY = mybir.ActivationFunctionType.Copy
+
+P = 128
+PACK = 4
+K_PASS = P * PACK
+B, S, D, H, DH = 2, 256, 2048, 16, 128
+EPS = 1e-6
+PASSES = D // K_PASS
+TOKEN_TILES = S // P
+GROUP_HEADS = 4
+GROUP_COLS = GROUP_HEADS * DH
+GROUPS = H // GROUP_HEADS
+GROUP_BANKS = B * TOKEN_TILES
+SUM_LAG = PASSES
+WORDS = K_PASS // 2
+VECTOR_COLS = 304
+
+FLOPS = 2 * B * S * D * H * DH
+
+
+def tile_multiheadattention_pa_kernel(tc, x, w, out):
+    nc = tc.nc
+    with ExitStack() as ctx:
+        keep = ctx.enter_context(tc.tile_pool(name="keep", bufs=1))
+        stage = ctx.enter_context(tc.tile_pool(name="stage", bufs=3))
+        results = ctx.enter_context(tc.tile_pool(name="results", bufs=GROUPS))
+        psum = ctx.enter_context(tc.psum_pool(name="psum", bufs=1))
+        ctx.enter_context(tc.manual_schedule())
+
+        ident = keep.tile([P, P], F32)
+        make_identity(nc, ident[:])
+
+        x_raw = keep.tile([P, B * TOKEN_TILES * D], BF16)
+        x_rows = x_raw[:].rearrange("p (b m k) -> p b m k", b=B, m=TOKEN_TILES)
+        x_words = x_raw[:].bitcast(F32).rearrange("p (b m q) -> p b m q", b=B, m=TOKEN_TILES)
+        x_grouped = keep.tile([P, B * PASSES * S * PACK], BF16, align_bytes=64)
+        x_grouped_cols = x_grouped[:].rearrange("p (b c) -> p b c", b=B)
+        x_grouped_words = x_grouped[:].bitcast(F32).rearrange(
+            "p (b g m r u) -> p b g m r u", b=B, g=PASSES, m=TOKEN_TILES, u=2
+        )
+        x_codes = keep.tile([P, B, PASSES * S], U32, align_bytes=64)
+        x_scales = keep.tile([P, B, PASSES * S], U8, align_bytes=64)
+
+        w_raw = keep.tile([P, GROUPS, PASSES, PACK, GROUP_COLS], BF16)
+        w_codes = keep.tile([P, GROUPS, PASSES, GROUP_COLS], U32, align_bytes=64)
+        w_scales = keep.tile([P, GROUPS, PASSES, GROUP_COLS], U8, align_bytes=64)
+
+        def bank(index, shape, name):
+            return psum.tile(shape, F32, tag="bank%d" % index, name=name)
+
+        def load_w(c, g):
+            nc.sync.dma_start(
+                out=w_raw[:, c, g],
+                in_=w[K_PASS * g : K_PASS * (g + 1), GROUP_COLS * c : GROUP_COLS * (c + 1)].rearrange("(p t) n -> p t n", t=PACK),
+            )
+
+        def load_x(b):
+            for half in range(2):
+                k_half = slice(D // 2 * half, D // 2 * (half + 1))
+                nc.sync.dma_start(
+                    out=x_rows[:, b, :, k_half], in_=x[b, :, k_half].rearrange("(p m) k -> p m k", m=TOKEN_TILES)
+                )
+
+        xt = {}
+
+        def turn_x(b, g):
+            xt[(b, g)] = bank(GROUP_BANKS * b + g, [P, TOKEN_TILES, 2, P], "xt")
+            for m in range(TOKEN_TILES):
+                for u in range(2):
+                    nc.tensor.transpose(
+                        xt[(b, g)][:, m, u, :], x_words[:, b, m, WORDS * g + u : WORDS * (g + 1) : 2], ident[:]
+                    )
+
+        def quantise_x(b, g):
+            nc.scalar.copy(out=x_grouped_words[:, b, g], in_=xt[(b, g)][:].rearrange("p m u r -> p m r u"))
+            nc.vector.quantize_mx(
+                out=x_codes[:, b, S * g : S * (g + 1)].bitcast(FP8X4),
+                scales=x_scales[:, b, S * g : S * (g + 1)],
+                in_=x_grouped_cols[:, b, S * PACK * g : S * PACK * (g + 1)],
+            )
+
+        grouped = {}
+
+        def regroup_w(c, g):
+            grouped[(c, g)] = stage.tile([P, GROUP_COLS, PACK], BF16, align_bytes=64, tag="grouped", name="grouped")
+            dst = grouped[(c, g)][:].rearrange("p (c i) t -> p c t i", i=4)
+            src = w_raw[:, c, g].rearrange("p t (c i) -> p c t i", i=4)
+            split = VECTOR_COLS // 4
+            nc.vector.tensor_copy(out=dst[:, :split], in_=src[:, :split])
+            nc.scalar.copy(out=dst[:, split:], in_=src[:, split:])
+
+        def quantise_w(c, g):
+            nc.vector.quantize_mx(
+                out=w_codes[:, c, g, :].bitcast(FP8X4),
+                scales=w_scales[:, c, g, :],
+                in_=grouped[(c, g)][:].rearrange("p n t -> p (n t)"),
+            )
+
+        acc = {}
+
+        def multiply(c, g, b):
+            for m in range(TOKEN_TILES):
+                if g == 0:
+                    acc[(c, b, m)] = bank(GROUP_BANKS * (c % 2) + TOKEN_TILES * b + m, [P, GROUP_COLS], "acc")
+                tokens = slice(S * g + P * m, S * g + P * (m + 1))
+                nc.tensor.matmul_mx(
+                    out=acc[(c, b, m)][:],
+                    lhsT=x_codes[:, b, tokens].bitcast(FP8X4),
+                    lhsT_scale=x_scales[:, b, tokens],
+                    rhs=w_codes[:, c, g, :].bitcast(FP8X4),
+                    rhs_scale=w_scales[:, c, g, :],
+                    start=(g == 0),
+                    stop=(g == PASSES - 1),
+                )
+
+        y = {}
+        sums = {}
+        inverse = {}
+
+        def sum_heads(c, b, m):
+            if b == 0 and m == 0:
+                y[c] = results.tile([P, B, GROUP_HEADS, TOKEN_TILES, DH], F32, tag="y", name="y")
+                sums[c] = results.tile([P, B, TOKEN_TILES, GROUP_HEADS], F32, tag="sums", name="sums")
+                inverse[c] = results.tile([P, B, TOKEN_TILES, GROUP_HEADS], F32, tag="inverse", name="inverse")
+            for h in range(GROUP_HEADS):
+                nc.scalar.activation(
+                    out=y[c][:, b, h, m, :],
+                    in_=acc[(c, b, m)][:, DH * h : DH * (h + 1)],
+                    func=COPY,
+                    accum_out=sums[c][:, b, m, h : h + 1],
+                )
+
+        def scale_and_store(c, b):
+            for m in range(TOKEN_TILES):
+                for h in range(GROUP_HEADS):
+                    nc.vector.tensor_scalar_mul(
+                        out=y[c][:, b, h, m, :], in0=y[c][:, b, h, m, :], scalar1=inverse[c][:, b, m, h : h + 1]
+                    )
+            nc.sync.dma_start(
+                out=out[b, GROUP_HEADS * c : GROUP_HEADS * (c + 1)].rearrange("h (p m) d -> p h (m d)", m=TOKEN_TILES),
+                in_=y[c][:, b].rearrange("p h m d -> p h (m d)"),
+            )
+
+        chunks = [(c, g) for c in range(GROUPS) for g in range(PASSES)]
+        units = [(c, b, m) for c in range(GROUPS) for b in range(B) for m in range(TOKEN_TILES)]
+
+        for b in range(B):
+            load_x(b)
+        for c, g in chunks:
+            load_w(c, g)
+
+        for b in range(B):
+            for g in range(PASSES):
+                turn_x(b, g)
+        for g in range(PASSES):
+            quantise_x(0, g)
+        regroup_w(0, 0)
+
+        for j in range(len(chunks) + SUM_LAG + 2):
+            if j < PASSES:
+                quantise_x(1, j)
+            summed = j - SUM_LAG - 1
+            finish = None
+            if 0 <= summed < len(units) and units[summed][2] == TOKEN_TILES - 1:
+                finish = units[summed][:2]
+            if finish:
+                nc.vector.tensor_scalar_add(out=inverse[finish[0]][:, finish[1]], in0=sums[finish[0]][:, finish[1]], scalar1=EPS)
+            if j < len(chunks):
+                c, g = chunks[j]
+                quantise_w(c, g)
+                for b in range(B):
+                    multiply(c, g, b)
+            if finish:
+                nc.vector.reciprocal(out=inverse[finish[0]][:, finish[1]], in_=inverse[finish[0]][:, finish[1]])
+            if j + 1 < len(chunks):
+                regroup_w(*chunks[j + 1])
+            if 0 <= j - SUM_LAG < len(units):
+                sum_heads(*units[j - SUM_LAG])
+            if finish:
+                scale_and_store(*finish)

@@ -20,8 +20,8 @@ TOKEN_TILES = S // P
 GROUP_HEADS = 4
 GROUP_COLS = GROUP_HEADS * DH
 GROUPS = H // GROUP_HEADS
-GROUP_BANKS = B * TOKEN_TILES
-SUM_LAG = PASSES
+GROUP_UNITS = B * TOKEN_TILES
+BANKS = 8
 WORDS = K_PASS // 2
 VECTOR_COLS = 304
 
@@ -32,7 +32,7 @@ def tile_multiheadattention_pa_kernel(tc, x, w, out):
     nc = tc.nc
     with ExitStack() as ctx:
         keep = ctx.enter_context(tc.tile_pool(name="keep", bufs=1))
-        stage = ctx.enter_context(tc.tile_pool(name="stage", bufs=3))
+        stage = ctx.enter_context(tc.tile_pool(name="stage", bufs=5))
         results = ctx.enter_context(tc.tile_pool(name="results", bufs=GROUPS))
         psum = ctx.enter_context(tc.psum_pool(name="psum", bufs=1))
         ctx.enter_context(tc.manual_schedule())
@@ -51,17 +51,21 @@ def tile_multiheadattention_pa_kernel(tc, x, w, out):
         x_codes = keep.tile([P, B, PASSES * S], U32, align_bytes=64)
         x_scales = keep.tile([P, B, PASSES * S], U8, align_bytes=64)
 
-        w_raw = keep.tile([P, GROUPS, PASSES, PACK, GROUP_COLS], BF16)
-        w_codes = keep.tile([P, GROUPS, PASSES, GROUP_COLS], U32, align_bytes=64)
-        w_scales = keep.tile([P, GROUPS, PASSES, GROUP_COLS], U8, align_bytes=64)
+        chunks = GROUPS * PASSES
+        w_raw = keep.tile([P, chunks, PACK, GROUP_COLS], BF16)
+        w_codes = keep.tile([P, chunks, GROUP_COLS], U32, align_bytes=64)
+        w_scales = keep.tile([P, chunks, GROUP_COLS], U8, align_bytes=64)
 
         def bank(index, shape, name):
             return psum.tile(shape, F32, tag="bank%d" % index, name=name)
 
-        def load_w(c, g):
+        def load_w(j):
+            c, g = divmod(j, PASSES)
             nc.sync.dma_start(
-                out=w_raw[:, c, g],
-                in_=w[K_PASS * g : K_PASS * (g + 1), GROUP_COLS * c : GROUP_COLS * (c + 1)].rearrange("(p t) n -> p t n", t=PACK),
+                out=w_raw[:, j],
+                in_=w[K_PASS * g : K_PASS * (g + 1), GROUP_COLS * c : GROUP_COLS * (c + 1)].rearrange(
+                    "(p t) n -> p t n", t=PACK
+                ),
             )
 
         def load_x(b):
@@ -74,7 +78,7 @@ def tile_multiheadattention_pa_kernel(tc, x, w, out):
         xt = {}
 
         def turn_x(b, g):
-            xt[(b, g)] = bank(GROUP_BANKS * b + g, [P, TOKEN_TILES, 2, P], "xt")
+            xt[(b, g)] = bank(PASSES * b + g, [P, TOKEN_TILES, 2, P], "xt")
             for m in range(TOKEN_TILES):
                 for u in range(2):
                     nc.tensor.transpose(
@@ -91,100 +95,126 @@ def tile_multiheadattention_pa_kernel(tc, x, w, out):
 
         grouped = {}
 
-        def regroup_w(c, g):
-            grouped[(c, g)] = stage.tile([P, GROUP_COLS, PACK], BF16, align_bytes=64, tag="grouped", name="grouped")
-            dst = grouped[(c, g)][:].rearrange("p (c i) t -> p c t i", i=4)
-            src = w_raw[:, c, g].rearrange("p t (c i) -> p c t i", i=4)
+        def regroup_w(j):
+            grouped[j] = stage.tile([P, GROUP_COLS, PACK], BF16, align_bytes=64, tag="grouped", name="grouped")
+            dst = grouped[j][:].rearrange("p (c i) t -> p c t i", i=4)
+            src = w_raw[:, j].rearrange("p t (c i) -> p c t i", i=4)
             split = VECTOR_COLS // 4
             nc.vector.tensor_copy(out=dst[:, :split], in_=src[:, :split])
             nc.scalar.copy(out=dst[:, split:], in_=src[:, split:])
 
-        def quantise_w(c, g):
+        def quantise_w(j):
             nc.vector.quantize_mx(
-                out=w_codes[:, c, g, :].bitcast(FP8X4),
-                scales=w_scales[:, c, g, :],
-                in_=grouped[(c, g)][:].rearrange("p n t -> p (n t)"),
+                out=w_codes[:, j, :].bitcast(FP8X4),
+                scales=w_scales[:, j, :],
+                in_=grouped[j][:].rearrange("p n t -> p (n t)"),
             )
 
         acc = {}
 
-        def multiply(c, g, b):
-            for m in range(TOKEN_TILES):
-                if g == 0:
-                    acc[(c, b, m)] = bank(GROUP_BANKS * (c % 2) + TOKEN_TILES * b + m, [P, GROUP_COLS], "acc")
-                tokens = slice(S * g + P * m, S * g + P * (m + 1))
-                nc.tensor.matmul_mx(
-                    out=acc[(c, b, m)][:],
-                    lhsT=x_codes[:, b, tokens].bitcast(FP8X4),
-                    lhsT_scale=x_scales[:, b, tokens],
-                    rhs=w_codes[:, c, g, :].bitcast(FP8X4),
-                    rhs_scale=w_scales[:, c, g, :],
-                    start=(g == 0),
-                    stop=(g == PASSES - 1),
-                )
+        def multiply(unit, g):
+            c, tile = divmod(unit, GROUP_UNITS)
+            b, m = divmod(tile, TOKEN_TILES)
+            if g == 0:
+                acc[unit] = bank(unit % BANKS, [P, GROUP_COLS], "acc")
+            tokens = slice(S * g + P * m, S * g + P * (m + 1))
+            nc.tensor.matmul_mx(
+                out=acc[unit][:],
+                lhsT=x_codes[:, b, tokens].bitcast(FP8X4),
+                lhsT_scale=x_scales[:, b, tokens],
+                rhs=w_codes[:, PASSES * c + g, :].bitcast(FP8X4),
+                rhs_scale=w_scales[:, PASSES * c + g, :],
+                start=(g == 0),
+                stop=(g == PASSES - 1),
+            )
 
         y = {}
         sums = {}
         inverse = {}
 
-        def sum_heads(c, b, m):
-            if b == 0 and m == 0:
-                y[c] = results.tile([P, B, GROUP_HEADS, TOKEN_TILES, DH], F32, tag="y", name="y")
-                sums[c] = results.tile([P, B, TOKEN_TILES, GROUP_HEADS], F32, tag="sums", name="sums")
-                inverse[c] = results.tile([P, B, TOKEN_TILES, GROUP_HEADS], F32, tag="inverse", name="inverse")
+        def sum_heads(unit):
+            pair, m = divmod(unit, TOKEN_TILES)
+            if m == 0:
+                y[pair] = results.tile([P, GROUP_HEADS, TOKEN_TILES, DH], F32, tag="y", name="y")
+                sums[pair] = results.tile([P, TOKEN_TILES, GROUP_HEADS], F32, tag="sums", name="sums")
+                inverse[pair] = results.tile([P, TOKEN_TILES, GROUP_HEADS], F32, tag="inverse", name="inverse")
             for h in range(GROUP_HEADS):
                 nc.scalar.activation(
-                    out=y[c][:, b, h, m, :],
-                    in_=acc[(c, b, m)][:, DH * h : DH * (h + 1)],
+                    out=y[pair][:, h, m, :],
+                    in_=acc[unit][:, DH * h : DH * (h + 1)],
                     func=COPY,
-                    accum_out=sums[c][:, b, m, h : h + 1],
+                    accum_out=sums[pair][:, m, h : h + 1],
                 )
 
-        def scale_and_store(c, b):
+        def add_eps(pair):
+            nc.vector.tensor_scalar_add(out=inverse[pair][:], in0=sums[pair][:], scalar1=EPS)
+
+        def invert(pair):
+            nc.vector.reciprocal(out=inverse[pair][:], in_=inverse[pair][:])
+
+        def scale_and_store(pair):
+            c, b = divmod(pair, B)
             for m in range(TOKEN_TILES):
                 for h in range(GROUP_HEADS):
                     nc.vector.tensor_scalar_mul(
-                        out=y[c][:, b, h, m, :], in0=y[c][:, b, h, m, :], scalar1=inverse[c][:, b, m, h : h + 1]
+                        out=y[pair][:, h, m, :], in0=y[pair][:, h, m, :], scalar1=inverse[pair][:, m, h : h + 1]
                     )
             nc.sync.dma_start(
                 out=out[b, GROUP_HEADS * c : GROUP_HEADS * (c + 1)].rearrange("h (p m) d -> p h (m d)", m=TOKEN_TILES),
-                in_=y[c][:, b].rearrange("p h m d -> p h (m d)"),
+                in_=y[pair][:].rearrange("p h m d -> p h (m d)"),
             )
 
-        chunks = [(c, g) for c in range(GROUPS) for g in range(PASSES)]
-        units = [(c, b, m) for c in range(GROUPS) for b in range(B) for m in range(TOKEN_TILES)]
+        units = GROUPS * GROUP_UNITS
+        passes_at = {}
+        finished_at = {}
+        for unit in range(units):
+            c, tile = divmod(unit, GROUP_UNITS)
+            late = tile if c < GROUPS - 1 else 0
+            for g in range(PASSES):
+                passes_at.setdefault(PASSES * c + g + late, []).append((unit, g))
+            finished_at.setdefault(PASSES * c + PASSES - 1 + late, []).append(unit)
 
+        for j in range(2):
+            load_w(j)
         for b in range(B):
             load_x(b)
-        for c, g in chunks:
-            load_w(c, g)
+        for j in range(2, chunks):
+            load_w(j)
 
-        for b in range(B):
-            for g in range(PASSES):
-                turn_x(b, g)
+        regroup_w(0)
+        regroup_w(1)
+        for g in range(PASSES):
+            turn_x(0, g)
+        quantise_w(0)
         for g in range(PASSES):
             quantise_x(0, g)
-        regroup_w(0, 0)
+        for g in range(PASSES):
+            turn_x(1, g)
+        regroup_w(2)
 
-        for j in range(len(chunks) + SUM_LAG + 2):
-            if j < PASSES:
-                quantise_x(1, j)
-            summed = j - SUM_LAG - 1
+        to_sum = []
+        to_finish = []
+        for j in range(chunks + 6):
+            if j + 1 < chunks:
+                quantise_w(j + 1)
+            if j < 2:
+                for g in range(2):
+                    quantise_x(1, 2 * j + g)
             finish = None
-            if 0 <= summed < len(units) and units[summed][2] == TOKEN_TILES - 1:
-                finish = units[summed][:2]
-            if finish:
-                nc.vector.tensor_scalar_add(out=inverse[finish[0]][:, finish[1]], in0=sums[finish[0]][:, finish[1]], scalar1=EPS)
-            if j < len(chunks):
-                c, g = chunks[j]
-                quantise_w(c, g)
-                for b in range(B):
-                    multiply(c, g, b)
-            if finish:
-                nc.vector.reciprocal(out=inverse[finish[0]][:, finish[1]], in_=inverse[finish[0]][:, finish[1]])
-            if j + 1 < len(chunks):
-                regroup_w(*chunks[j + 1])
-            if 0 <= j - SUM_LAG < len(units):
-                sum_heads(*units[j - SUM_LAG])
-            if finish:
-                scale_and_store(*finish)
+            if to_finish:
+                finish = to_finish.pop(0)
+                add_eps(finish)
+            for unit, g in passes_at.get(j, []):
+                multiply(unit, g)
+            if j + 3 < chunks:
+                regroup_w(j + 3)
+            if finish is not None:
+                invert(finish)
+            if to_sum:
+                unit = to_sum.pop(0)
+                sum_heads(unit)
+                if unit % TOKEN_TILES == TOKEN_TILES - 1:
+                    to_finish.append(unit // TOKEN_TILES)
+            to_sum.extend(finished_at.get(j, []))
+            if finish is not None:
+                scale_and_store(finish)

@@ -17,13 +17,17 @@ B, S, D, H, DH = 2, 256, 2048, 16, 128
 EPS = 1e-6
 PASSES = D // K_PASS
 TOKEN_TILES = S // P
-GROUP_HEADS = 4
-GROUP_COLS = GROUP_HEADS * DH
-GROUPS = H // GROUP_HEADS
+GROUP_HEADS = (4, 4, 4, 2, 2)
+GROUPS = len(GROUP_HEADS)
+FIRST_HEAD = [sum(GROUP_HEADS[:c]) for c in range(GROUPS)]
+LOAD_HEADS = 4
 GROUP_UNITS = B * TOKEN_TILES
 BANKS = 8
 WORDS = K_PASS // 2
-VECTOR_COLS = 304
+VECTOR_X = ()
+EARLY_SHARE = 24
+EARLY_CHUNKS = 4
+VECTOR_SHARE = 20
 
 FLOPS = 2 * B * S * D * H * DH
 
@@ -40,9 +44,7 @@ def tile_multiheadattention_pa_kernel(tc, x, w, out):
         ident = keep.tile([P, P], F32)
         make_identity(nc, ident[:])
 
-        x_raw = keep.tile([P, B * TOKEN_TILES * D], BF16)
-        x_rows = x_raw[:].rearrange("p (b m k) -> p b m k", b=B, m=TOKEN_TILES)
-        x_words = x_raw[:].bitcast(F32).rearrange("p (b m q) -> p b m q", b=B, m=TOKEN_TILES)
+        x_raw = {}
         x_grouped = keep.tile([P, B * PASSES * S * PACK], BF16, align_bytes=64)
         x_grouped_cols = x_grouped[:].rearrange("p (b c) -> p b c", b=B)
         x_grouped_words = x_grouped[:].bitcast(F32).rearrange(
@@ -52,41 +54,50 @@ def tile_multiheadattention_pa_kernel(tc, x, w, out):
         x_scales = keep.tile([P, B, PASSES * S], U8, align_bytes=64)
 
         chunks = GROUPS * PASSES
-        w_raw = keep.tile([P, chunks, PACK, GROUP_COLS], BF16)
-        w_codes = keep.tile([P, chunks, GROUP_COLS], U32, align_bytes=64)
-        w_scales = keep.tile([P, chunks, GROUP_COLS], U8, align_bytes=64)
+        w_raw = {}
+        w_codes = keep.tile([P, PASSES, H * DH], U32, align_bytes=64)
+        w_scales = keep.tile([P, PASSES, H * DH], U8, align_bytes=64)
+
+        def chunk_cols(j):
+            c = j // PASSES
+            return slice(DH * FIRST_HEAD[c], DH * (FIRST_HEAD[c] + GROUP_HEADS[c]))
 
         def bank(index, shape, name):
             return psum.tile(shape, F32, tag="bank%d" % index, name=name)
 
-        def load_w(j):
-            c, g = divmod(j, PASSES)
+        def load_w(g, h0):
+            raw = keep.tile([P, PACK, LOAD_HEADS * DH], BF16, name="raw_%d_%d" % (g, h0))
             nc.sync.dma_start(
-                out=w_raw[:, j],
-                in_=w[K_PASS * g : K_PASS * (g + 1), GROUP_COLS * c : GROUP_COLS * (c + 1)].rearrange(
-                    "(p t) n -> p t n", t=PACK
-                ),
+                out=raw[:],
+                in_=w[K_PASS * g : K_PASS * (g + 1), DH * h0 : DH * (h0 + LOAD_HEADS)].rearrange("(p t) n -> p t n", t=PACK),
             )
+            for c in range(GROUPS):
+                if h0 <= FIRST_HEAD[c] < h0 + LOAD_HEADS:
+                    n0 = DH * (FIRST_HEAD[c] - h0)
+                    w_raw[PASSES * c + g] = raw[:, :, n0 : n0 + DH * GROUP_HEADS[c]]
 
         def load_x(b):
             for half in range(2):
                 k_half = slice(D // 2 * half, D // 2 * (half + 1))
-                nc.sync.dma_start(
-                    out=x_rows[:, b, :, k_half], in_=x[b, :, k_half].rearrange("(p m) k -> p m k", m=TOKEN_TILES)
-                )
+                raw = keep.tile([P, TOKEN_TILES, D // 2], BF16, name="x_%d_%d" % (b, half))
+                nc.sync.dma_start(out=raw[:], in_=x[b, :, k_half].rearrange("(p m) k -> p m k", m=TOKEN_TILES))
+                x_raw[(b, half)] = raw[:].bitcast(F32)
 
         xt = {}
 
         def turn_x(b, g):
             xt[(b, g)] = bank(PASSES * b + g, [P, TOKEN_TILES, 2, P], "xt")
+            half, part = divmod(g, PASSES // 2)
             for m in range(TOKEN_TILES):
                 for u in range(2):
-                    nc.tensor.transpose(
-                        xt[(b, g)][:, m, u, :], x_words[:, b, m, WORDS * g + u : WORDS * (g + 1) : 2], ident[:]
-                    )
+                    words = x_raw[(b, half)][:, m, WORDS * part + u : WORDS * (part + 1) : 2]
+                    nc.tensor.transpose(xt[(b, g)][:, m, u, :], words, ident[:])
+
+        def empty_x(b, g):
+            copy = nc.vector.tensor_copy if (b, g) in VECTOR_X else nc.scalar.copy
+            copy(out=x_grouped_words[:, b, g], in_=xt[(b, g)][:].rearrange("p m u r -> p m r u"))
 
         def quantise_x(b, g):
-            nc.scalar.copy(out=x_grouped_words[:, b, g], in_=xt[(b, g)][:].rearrange("p m u r -> p m r u"))
             nc.vector.quantize_mx(
                 out=x_codes[:, b, S * g : S * (g + 1)].bitcast(FP8X4),
                 scales=x_scales[:, b, S * g : S * (g + 1)],
@@ -96,19 +107,23 @@ def tile_multiheadattention_pa_kernel(tc, x, w, out):
         grouped = {}
 
         def regroup_w(j):
-            grouped[j] = stage.tile([P, GROUP_COLS, PACK], BF16, align_bytes=64, tag="grouped", name="grouped")
+            if j >= chunks:
+                return
+            cols = DH * GROUP_HEADS[j // PASSES]
+            grouped[j] = stage.tile([P, cols, PACK], BF16, align_bytes=64, tag="grouped", name="grouped")
             dst = grouped[j][:].rearrange("p (c i) t -> p c t i", i=4)
-            src = w_raw[:, j].rearrange("p t (c i) -> p c t i", i=4)
-            split = VECTOR_COLS // 4
+            src = w_raw[j].rearrange("p t (c i) -> p c t i", i=4)
+            split = cols // 32 * (EARLY_SHARE if j < EARLY_CHUNKS else VECTOR_SHARE) // 8 * 2
             nc.vector.tensor_copy(out=dst[:, :split], in_=src[:, :split])
             nc.scalar.copy(out=dst[:, split:], in_=src[:, split:])
 
         def quantise_w(j):
-            nc.vector.quantize_mx(
-                out=w_codes[:, j, :].bitcast(FP8X4),
-                scales=w_scales[:, j, :],
-                in_=grouped[j][:].rearrange("p n t -> p (n t)"),
-            )
+            if j < chunks:
+                nc.vector.quantize_mx(
+                    out=w_codes[:, j % PASSES, chunk_cols(j)].bitcast(FP8X4),
+                    scales=w_scales[:, j % PASSES, chunk_cols(j)],
+                    in_=grouped[j][:].rearrange("p n t -> p (n t)"),
+                )
 
         acc = {}
 
@@ -116,14 +131,14 @@ def tile_multiheadattention_pa_kernel(tc, x, w, out):
             c, tile = divmod(unit, GROUP_UNITS)
             b, m = divmod(tile, TOKEN_TILES)
             if g == 0:
-                acc[unit] = bank(unit % BANKS, [P, GROUP_COLS], "acc")
+                acc[unit] = bank(unit % BANKS, [P, DH * GROUP_HEADS[c]], "acc")
             tokens = slice(S * g + P * m, S * g + P * (m + 1))
             nc.tensor.matmul_mx(
                 out=acc[unit][:],
                 lhsT=x_codes[:, b, tokens].bitcast(FP8X4),
                 lhsT_scale=x_scales[:, b, tokens],
-                rhs=w_codes[:, PASSES * c + g, :].bitcast(FP8X4),
-                rhs_scale=w_scales[:, PASSES * c + g, :],
+                rhs=w_codes[:, g, chunk_cols(PASSES * c)].bitcast(FP8X4),
+                rhs_scale=w_scales[:, g, chunk_cols(PASSES * c)],
                 start=(g == 0),
                 stop=(g == PASSES - 1),
             )
@@ -134,11 +149,12 @@ def tile_multiheadattention_pa_kernel(tc, x, w, out):
 
         def sum_heads(unit):
             pair, m = divmod(unit, TOKEN_TILES)
+            heads = GROUP_HEADS[pair // B]
             if m == 0:
-                y[pair] = results.tile([P, GROUP_HEADS, TOKEN_TILES, DH], F32, tag="y", name="y")
-                sums[pair] = results.tile([P, TOKEN_TILES, GROUP_HEADS], F32, tag="sums", name="sums")
-                inverse[pair] = results.tile([P, TOKEN_TILES, GROUP_HEADS], F32, tag="inverse", name="inverse")
-            for h in range(GROUP_HEADS):
+                y[pair] = results.tile([P, heads, TOKEN_TILES, DH], F32, tag="y", name="y")
+                sums[pair] = results.tile([P, TOKEN_TILES, heads], F32, tag="sums", name="sums")
+                inverse[pair] = results.tile([P, TOKEN_TILES, heads], F32, tag="inverse", name="inverse")
+            for h in range(heads):
                 nc.scalar.activation(
                     out=y[pair][:, h, m, :],
                     in_=acc[unit][:, DH * h : DH * (h + 1)],
@@ -155,12 +171,14 @@ def tile_multiheadattention_pa_kernel(tc, x, w, out):
         def scale_and_store(pair):
             c, b = divmod(pair, B)
             for m in range(TOKEN_TILES):
-                for h in range(GROUP_HEADS):
+                for h in range(GROUP_HEADS[c]):
                     nc.vector.tensor_scalar_mul(
                         out=y[pair][:, h, m, :], in0=y[pair][:, h, m, :], scalar1=inverse[pair][:, m, h : h + 1]
                     )
             nc.sync.dma_start(
-                out=out[b, GROUP_HEADS * c : GROUP_HEADS * (c + 1)].rearrange("h (p m) d -> p h (m d)", m=TOKEN_TILES),
+                out=out[b, FIRST_HEAD[c] : FIRST_HEAD[c] + GROUP_HEADS[c]].rearrange(
+                    "h (p m) d -> p h (m d)", m=TOKEN_TILES
+                ),
                 in_=y[pair][:].rearrange("p h m d -> p h (m d)"),
             )
 
@@ -174,42 +192,60 @@ def tile_multiheadattention_pa_kernel(tc, x, w, out):
                 passes_at.setdefault(PASSES * c + g + late, []).append((unit, g))
             finished_at.setdefault(PASSES * c + PASSES - 1 + late, []).append(unit)
 
-        for j in range(2):
-            load_w(j)
-        for b in range(B):
-            load_x(b)
-        for j in range(2, chunks):
-            load_w(j)
+        loads = [(g, h0) for h0 in range(0, H, LOAD_HEADS) for g in range(PASSES)]
+        load_w(*loads[0])
+        load_w(*loads[1])
+        load_x(0)
+        load_w(*loads[2])
+        load_x(1)
+        for g, h0 in loads[3:]:
+            load_w(g, h0)
 
+        for b in range(B):
+            for g in range(PASSES):
+                turn_x(b, g)
         regroup_w(0)
         regroup_w(1)
-        for g in range(PASSES):
-            turn_x(0, g)
         quantise_w(0)
-        for g in range(PASSES):
-            quantise_x(0, g)
-        for g in range(PASSES):
-            turn_x(1, g)
+        quantise_w(1)
+        empty_x(0, 0)
+        empty_x(0, 1)
+        quantise_x(0, 0)
+        empty_x(0, 2)
+        quantise_x(0, 1)
+        empty_x(0, 3)
         regroup_w(2)
+        quantise_x(0, 2)
+        quantise_x(0, 3)
+        quantise_w(2)
+        empty_x(1, 0)
+        empty_x(1, 1)
+        quantise_x(1, 0)
+        empty_x(1, 2)
+        quantise_x(1, 1)
+        empty_x(1, 3)
+        regroup_w(3)
+        quantise_x(1, 2)
+        quantise_x(1, 3)
+        regroup_w(4)
 
         to_sum = []
         to_finish = []
         for j in range(chunks + 6):
-            if j + 1 < chunks:
-                quantise_w(j + 1)
-            if j < 2:
-                for g in range(2):
-                    quantise_x(1, 2 * j + g)
             finish = None
             if to_finish:
                 finish = to_finish.pop(0)
                 add_eps(finish)
-            for unit, g in passes_at.get(j, []):
-                multiply(unit, g)
-            if j + 3 < chunks:
-                regroup_w(j + 3)
+            if 1 < j < chunks - 2:
+                quantise_w(j + 1)
+            if j == chunks - 3:
+                quantise_w(j + 2)
             if finish is not None:
                 invert(finish)
+            for unit, g in passes_at.get(j, []):
+                multiply(unit, g)
+            if j > 1:
+                regroup_w(j + 3)
             if to_sum:
                 unit = to_sum.pop(0)
                 sum_heads(unit)

@@ -17,16 +17,15 @@ B, S, D, H, DH = 2, 256, 2048, 16, 128
 EPS = 1e-6
 PASSES = D // K_PASS
 TOKEN_TILES = S // P
-GROUP_HEADS = (4, 4, 4, 2, 2)
+GROUP_HEADS = (4, 4, 4, 2, 1, 1)
 GROUPS = len(GROUP_HEADS)
 FIRST_HEAD = [sum(GROUP_HEADS[:c]) for c in range(GROUPS)]
 LOAD_HEADS = 4
 GROUP_UNITS = B * TOKEN_TILES
 BANKS = 8
 WORDS = K_PASS // 2
-VECTOR_X = ()
-EARLY_SHARE = 24
 EARLY_CHUNKS = 4
+EARLY_SHARE = 24
 VECTOR_SHARE = 20
 
 FLOPS = 2 * B * S * D * H * DH
@@ -37,7 +36,7 @@ def tile_multiheadattention_pa_kernel(tc, x, w, out):
     with ExitStack() as ctx:
         keep = ctx.enter_context(tc.tile_pool(name="keep", bufs=1))
         stage = ctx.enter_context(tc.tile_pool(name="stage", bufs=5))
-        results = ctx.enter_context(tc.tile_pool(name="results", bufs=GROUPS))
+        results = ctx.enter_context(tc.tile_pool(name="results", bufs=B * GROUPS))
         psum = ctx.enter_context(tc.psum_pool(name="psum", bufs=1))
         ctx.enter_context(tc.manual_schedule())
 
@@ -45,13 +44,11 @@ def tile_multiheadattention_pa_kernel(tc, x, w, out):
         make_identity(nc, ident[:])
 
         x_raw = {}
-        x_grouped = keep.tile([P, B * PASSES * S * PACK], BF16, align_bytes=64)
-        x_grouped_cols = x_grouped[:].rearrange("p (b c) -> p b c", b=B)
-        x_grouped_words = x_grouped[:].bitcast(F32).rearrange(
-            "p (b g m r u) -> p b g m r u", b=B, g=PASSES, m=TOKEN_TILES, u=2
-        )
-        x_codes = keep.tile([P, B, PASSES * S], U32, align_bytes=64)
-        x_scales = keep.tile([P, B, PASSES * S], U8, align_bytes=64)
+        x_grouped = keep.tile([P, GROUP_UNITS * PASSES * P * PACK], BF16, align_bytes=64)
+        x_grouped_cols = x_grouped[:].rearrange("p (i c) -> p i c", i=GROUP_UNITS)
+        x_grouped_words = x_grouped[:].bitcast(F32).rearrange("p (i g r u) -> p i g r u", i=GROUP_UNITS, g=PASSES, u=2)
+        x_codes = keep.tile([P, GROUP_UNITS, PASSES * P], U32, align_bytes=64)
+        x_scales = keep.tile([P, GROUP_UNITS, PASSES * P], U8, align_bytes=64)
 
         chunks = GROUPS * PASSES
         w_raw = {}
@@ -67,42 +64,35 @@ def tile_multiheadattention_pa_kernel(tc, x, w, out):
 
         def load_w(g, h0):
             raw = keep.tile([P, PACK, LOAD_HEADS * DH], BF16, name="raw_%d_%d" % (g, h0))
-            nc.sync.dma_start(
-                out=raw[:],
-                in_=w[K_PASS * g : K_PASS * (g + 1), DH * h0 : DH * (h0 + LOAD_HEADS)].rearrange("(p t) n -> p t n", t=PACK),
-            )
+            rows = w[K_PASS * g : K_PASS * (g + 1), DH * h0 : DH * (h0 + LOAD_HEADS)]
+            nc.sync.dma_start(out=raw[:], in_=rows.rearrange("(p t) n -> p t n", t=PACK))
             for c in range(GROUPS):
                 if h0 <= FIRST_HEAD[c] < h0 + LOAD_HEADS:
                     n0 = DH * (FIRST_HEAD[c] - h0)
                     w_raw[PASSES * c + g] = raw[:, :, n0 : n0 + DH * GROUP_HEADS[c]]
 
-        def load_x(b):
-            for half in range(2):
-                k_half = slice(D // 2 * half, D // 2 * (half + 1))
-                raw = keep.tile([P, TOKEN_TILES, D // 2], BF16, name="x_%d_%d" % (b, half))
-                nc.sync.dma_start(out=raw[:], in_=x[b, :, k_half].rearrange("(p m) k -> p m k", m=TOKEN_TILES))
-                x_raw[(b, half)] = raw[:].bitcast(F32)
+        def load_x(i):
+            b, m = divmod(i, TOKEN_TILES)
+            raw = keep.tile([P, D], BF16, name="x_%d" % i)
+            nc.sync.dma_start(out=raw[:], in_=x[b].rearrange("(p m) k -> p m k", m=TOKEN_TILES)[:, m, :])
+            x_raw[i] = raw[:].bitcast(F32)
 
         xt = {}
 
-        def turn_x(b, g):
-            xt[(b, g)] = bank(PASSES * b + g, [P, TOKEN_TILES, 2, P], "xt")
-            half, part = divmod(g, PASSES // 2)
-            for m in range(TOKEN_TILES):
+        def turn_x(i, half):
+            xt[(i, half)] = bank(TOKEN_TILES * i + half, [P, 2, 2, P], "xt")
+            for part in range(2):
                 for u in range(2):
-                    words = x_raw[(b, half)][:, m, WORDS * part + u : WORDS * (part + 1) : 2]
-                    nc.tensor.transpose(xt[(b, g)][:, m, u, :], words, ident[:])
+                    g = 2 * half + part
+                    nc.tensor.transpose(xt[(i, half)][:, part, u, :], x_raw[i][:, WORDS * g + u : WORDS * (g + 1) : 2], ident[:])
 
-        def empty_x(b, g):
-            copy = nc.vector.tensor_copy if (b, g) in VECTOR_X else nc.scalar.copy
-            copy(out=x_grouped_words[:, b, g], in_=xt[(b, g)][:].rearrange("p m u r -> p m r u"))
-
-        def quantise_x(b, g):
-            nc.vector.quantize_mx(
-                out=x_codes[:, b, S * g : S * (g + 1)].bitcast(FP8X4),
-                scales=x_scales[:, b, S * g : S * (g + 1)],
-                in_=x_grouped_cols[:, b, S * PACK * g : S * PACK * (g + 1)],
+        def empty_x(i, half):
+            nc.scalar.copy(
+                out=x_grouped_words[:, i, 2 * half : 2 * half + 2], in_=xt[(i, half)][:].rearrange("p g u r -> p g r u")
             )
+
+        def quantise_x(i):
+            nc.vector.quantize_mx(out=x_codes[:, i, :].bitcast(FP8X4), scales=x_scales[:, i, :], in_=x_grouped_cols[:, i, :])
 
         grouped = {}
 
@@ -129,14 +119,13 @@ def tile_multiheadattention_pa_kernel(tc, x, w, out):
 
         def multiply(unit, g):
             c, tile = divmod(unit, GROUP_UNITS)
-            b, m = divmod(tile, TOKEN_TILES)
             if g == 0:
                 acc[unit] = bank(unit % BANKS, [P, DH * GROUP_HEADS[c]], "acc")
-            tokens = slice(S * g + P * m, S * g + P * (m + 1))
+            tokens = slice(P * g, P * (g + 1))
             nc.tensor.matmul_mx(
                 out=acc[unit][:],
-                lhsT=x_codes[:, b, tokens].bitcast(FP8X4),
-                lhsT_scale=x_scales[:, b, tokens],
+                lhsT=x_codes[:, tile, tokens].bitcast(FP8X4),
+                lhsT_scale=x_scales[:, tile, tokens],
                 rhs=w_codes[:, g, chunk_cols(PASSES * c)].bitcast(FP8X4),
                 rhs_scale=w_scales[:, g, chunk_cols(PASSES * c)],
                 start=(g == 0),
@@ -182,6 +171,7 @@ def tile_multiheadattention_pa_kernel(tc, x, w, out):
                 in_=y[pair][:].rearrange("p h m d -> p h (m d)"),
             )
 
+
         units = GROUPS * GROUP_UNITS
         passes_at = {}
         finished_at = {}
@@ -196,61 +186,52 @@ def tile_multiheadattention_pa_kernel(tc, x, w, out):
         load_w(*loads[0])
         load_w(*loads[1])
         load_x(0)
-        load_w(*loads[2])
         load_x(1)
+        load_w(*loads[2])
+        load_x(2)
+        load_x(3)
         for g, h0 in loads[3:]:
             load_w(g, h0)
 
-        for b in range(B):
-            for g in range(PASSES):
-                turn_x(b, g)
+        for i in range(GROUP_UNITS):
+            for half in range(2):
+                turn_x(i, half)
         regroup_w(0)
         regroup_w(1)
         quantise_w(0)
         quantise_w(1)
-        empty_x(0, 0)
-        empty_x(0, 1)
-        quantise_x(0, 0)
-        empty_x(0, 2)
-        quantise_x(0, 1)
-        empty_x(0, 3)
-        regroup_w(2)
-        quantise_x(0, 2)
-        quantise_x(0, 3)
-        quantise_w(2)
-        empty_x(1, 0)
-        empty_x(1, 1)
-        quantise_x(1, 0)
-        empty_x(1, 2)
-        quantise_x(1, 1)
-        empty_x(1, 3)
-        regroup_w(3)
-        quantise_x(1, 2)
-        quantise_x(1, 3)
+        for i in range(GROUP_UNITS):
+            for half in range(2):
+                empty_x(i, half)
+            if i % 2 == 1:
+                quantise_x(i - 1)
+                regroup_w(2 + i // 2)
+                quantise_x(i)
+            if i == 1:
+                quantise_w(2)
         regroup_w(4)
 
         to_sum = []
         to_finish = []
         for j in range(chunks + 6):
-            finish = None
-            if to_finish:
-                finish = to_finish.pop(0)
-                add_eps(finish)
+            finish = [pair for step, pair in to_finish if step == j]
+            for pair in finish:
+                add_eps(pair)
             if 1 < j < chunks - 2:
                 quantise_w(j + 1)
             if j == chunks - 3:
                 quantise_w(j + 2)
-            if finish is not None:
-                invert(finish)
+            for pair in finish:
+                invert(pair)
             for unit, g in passes_at.get(j, []):
                 multiply(unit, g)
             if j > 1:
                 regroup_w(j + 3)
-            if to_sum:
-                unit = to_sum.pop(0)
+            summed = to_sum[: GROUP_UNITS if j >= chunks - 1 else 1]
+            for unit in summed:
                 sum_heads(unit)
                 if unit % TOKEN_TILES == TOKEN_TILES - 1:
-                    to_finish.append(unit // TOKEN_TILES)
-            to_sum.extend(finished_at.get(j, []))
-            if finish is not None:
-                scale_and_store(finish)
+                    to_finish.append((j + (2 if j < chunks - 1 else 1), unit // TOKEN_TILES))
+            to_sum = to_sum[len(summed) :] + finished_at.get(j, [])
+            for pair in finish:
+                scale_and_store(pair)

@@ -17,16 +17,17 @@ B, S, D, H, DH = 2, 256, 2048, 16, 128
 EPS = 1e-6
 PASSES = D // K_PASS
 TOKEN_TILES = S // P
-GROUP_HEADS = (4, 4, 4, 2, 1, 1)
+BLOCKS = ((4, 2), (4, 2), (2,), (1,), (1,))
+GROUP_HEADS = sum(BLOCKS, ())
 GROUPS = len(GROUP_HEADS)
 FIRST_HEAD = [sum(GROUP_HEADS[:c]) for c in range(GROUPS)]
-LOAD_HEADS = 4
+LOAD_HEADS = (6, 6, 4)
 GROUP_UNITS = B * TOKEN_TILES
 BANKS = 8
 WORDS = K_PASS // 2
-EARLY_CHUNKS = 4
-EARLY_SHARE = 24
-VECTOR_SHARE = 20
+EARLY_STEPS = 12
+EARLY_SHARE = 18
+VECTOR_SHARE = 21
 
 FLOPS = 2 * B * S * D * H * DH
 
@@ -51,6 +52,10 @@ def tile_multiheadattention_pa_kernel(tc, x, w, out):
         x_scales = keep.tile([P, GROUP_UNITS, PASSES * P], U8, align_bytes=64)
 
         chunks = GROUPS * PASSES
+        order = []
+        for block in BLOCKS:
+            first = len(order) // PASSES
+            order.extend(PASSES * c + g for g in range(PASSES) for c in range(first, first + len(block)))
         w_raw = {}
         w_codes = keep.tile([P, PASSES, H * DH], U32, align_bytes=64)
         w_scales = keep.tile([P, PASSES, H * DH], U8, align_bytes=64)
@@ -62,12 +67,12 @@ def tile_multiheadattention_pa_kernel(tc, x, w, out):
         def bank(index, shape, name):
             return psum.tile(shape, F32, tag="bank%d" % index, name=name)
 
-        def load_w(g, h0):
-            raw = keep.tile([P, PACK, LOAD_HEADS * DH], BF16, name="raw_%d_%d" % (g, h0))
-            rows = w[K_PASS * g : K_PASS * (g + 1), DH * h0 : DH * (h0 + LOAD_HEADS)]
+        def load_w(g, h0, heads):
+            raw = keep.tile([P, PACK, heads * DH], BF16, name="raw_%d_%d" % (g, h0))
+            rows = w[K_PASS * g : K_PASS * (g + 1), DH * h0 : DH * (h0 + heads)]
             nc.sync.dma_start(out=raw[:], in_=rows.rearrange("(p t) n -> p t n", t=PACK))
             for c in range(GROUPS):
-                if h0 <= FIRST_HEAD[c] < h0 + LOAD_HEADS:
+                if h0 <= FIRST_HEAD[c] < h0 + heads:
                     n0 = DH * (FIRST_HEAD[c] - h0)
                     w_raw[PASSES * c + g] = raw[:, :, n0 : n0 + DH * GROUP_HEADS[c]]
 
@@ -96,24 +101,25 @@ def tile_multiheadattention_pa_kernel(tc, x, w, out):
 
         grouped = {}
 
-        def regroup_w(j):
-            if j >= chunks:
+        def regroup_w(step):
+            if step >= chunks:
                 return
+            j = order[step]
             cols = DH * GROUP_HEADS[j // PASSES]
             grouped[j] = stage.tile([P, cols, PACK], BF16, align_bytes=64, tag="grouped", name="grouped")
             dst = grouped[j][:].rearrange("p (c i) t -> p c t i", i=4)
             src = w_raw[j].rearrange("p t (c i) -> p c t i", i=4)
-            split = cols // 32 * (EARLY_SHARE if j < EARLY_CHUNKS else VECTOR_SHARE) // 8 * 2
+            split = cols // 32 * (EARLY_SHARE if step < EARLY_STEPS else VECTOR_SHARE) // 8 * 2
             nc.vector.tensor_copy(out=dst[:, :split], in_=src[:, :split])
             nc.scalar.copy(out=dst[:, split:], in_=src[:, split:])
 
-        def quantise_w(j):
-            if j < chunks:
-                nc.vector.quantize_mx(
-                    out=w_codes[:, j % PASSES, chunk_cols(j)].bitcast(FP8X4),
-                    scales=w_scales[:, j % PASSES, chunk_cols(j)],
-                    in_=grouped[j][:].rearrange("p n t -> p (n t)"),
-                )
+        def quantise_w(step):
+            j = order[step]
+            nc.vector.quantize_mx(
+                out=w_codes[:, j % PASSES, chunk_cols(j)].bitcast(FP8X4),
+                scales=w_scales[:, j % PASSES, chunk_cols(j)],
+                in_=grouped[j][:].rearrange("p n t -> p (n t)"),
+            )
 
         acc = {}
 
@@ -172,26 +178,17 @@ def tile_multiheadattention_pa_kernel(tc, x, w, out):
             )
 
 
-        units = GROUPS * GROUP_UNITS
-        passes_at = {}
-        finished_at = {}
-        for unit in range(units):
-            c, tile = divmod(unit, GROUP_UNITS)
-            late = tile if c < GROUPS - 1 else 0
-            for g in range(PASSES):
-                passes_at.setdefault(PASSES * c + g + late, []).append((unit, g))
-            finished_at.setdefault(PASSES * c + PASSES - 1 + late, []).append(unit)
-
-        loads = [(g, h0) for h0 in range(0, H, LOAD_HEADS) for g in range(PASSES)]
+        loads = []
+        for i, heads in enumerate(LOAD_HEADS):
+            loads.extend((g, sum(LOAD_HEADS[:i]), heads) for g in range(PASSES))
         load_w(*loads[0])
-        load_w(*loads[1])
         load_x(0)
         load_x(1)
-        load_w(*loads[2])
+        load_w(*loads[1])
         load_x(2)
         load_x(3)
-        for g, h0 in loads[3:]:
-            load_w(g, h0)
+        for g, h0, heads in loads[2:]:
+            load_w(g, h0, heads)
 
         for i in range(GROUP_UNITS):
             for half in range(2):
@@ -223,7 +220,9 @@ def tile_multiheadattention_pa_kernel(tc, x, w, out):
                 quantise_w(j + 2)
             for pair in finish:
                 invert(pair)
-            for unit, g in passes_at.get(j, []):
+            c, g = divmod(order[j], PASSES) if j < chunks else (0, -1)
+            units = range(GROUP_UNITS * c, GROUP_UNITS * (c + 1)) if j < chunks else ()
+            for unit in units:
                 multiply(unit, g)
             if j > 1:
                 regroup_w(j + 3)
@@ -232,6 +231,6 @@ def tile_multiheadattention_pa_kernel(tc, x, w, out):
                 sum_heads(unit)
                 if unit % TOKEN_TILES == TOKEN_TILES - 1:
                     to_finish.append((j + (2 if j < chunks - 1 else 1), unit // TOKEN_TILES))
-            to_sum = to_sum[len(summed) :] + finished_at.get(j, [])
+            to_sum = to_sum[len(summed) :] + (list(units) if g == PASSES - 1 else [])
             for pair in finish:
                 scale_and_store(pair)

@@ -25,9 +25,11 @@ LOAD_HEADS = (6, 6, 4)
 GROUP_UNITS = B * TOKEN_TILES
 BANKS = 8
 WORDS = K_PASS // 2
-EARLY_STEPS = 12
+WARM_MATMULS = 5
+WARM_COLS = 512
+EARLY_STEPS = 8
 EARLY_SHARE = 18
-VECTOR_SHARE = 21
+VECTOR_SHARE = 20
 
 FLOPS = 2 * B * S * D * H * DH
 
@@ -45,6 +47,7 @@ def tile_multiheadattention_pa_kernel(tc, x, w, out):
         make_identity(nc, ident[:])
 
         x_raw = {}
+        x_bf16 = {}
         x_grouped = keep.tile([P, GROUP_UNITS * PASSES * P * PACK], BF16, align_bytes=64)
         x_grouped_cols = x_grouped[:].rearrange("p (i c) -> p i c", i=GROUP_UNITS)
         x_grouped_words = x_grouped[:].bitcast(F32).rearrange("p (i g r u) -> p i g r u", i=GROUP_UNITS, g=PASSES, u=2)
@@ -80,6 +83,7 @@ def tile_multiheadattention_pa_kernel(tc, x, w, out):
             b, m = divmod(i, TOKEN_TILES)
             raw = keep.tile([P, D], BF16, name="x_%d" % i)
             nc.sync.dma_start(out=raw[:], in_=x[b].rearrange("(p m) k -> p m k", m=TOKEN_TILES)[:, m, :])
+            x_bf16[i] = raw
             x_raw[i] = raw[:].bitcast(F32)
 
         xt = {}
@@ -126,7 +130,7 @@ def tile_multiheadattention_pa_kernel(tc, x, w, out):
         def multiply(unit, g):
             c, tile = divmod(unit, GROUP_UNITS)
             if g == 0:
-                acc[unit] = bank(unit % BANKS, [P, DH * GROUP_HEADS[c]], "acc")
+                acc[unit] = bank(bank_of[unit], [P, DH * GROUP_HEADS[c]], "acc")
             tokens = slice(P * g, P * (g + 1))
             nc.tensor.matmul_mx(
                 out=acc[unit][:],
@@ -178,6 +182,23 @@ def tile_multiheadattention_pa_kernel(tc, x, w, out):
             )
 
 
+        passes_at = {}
+        finished_at = {}
+        starts = []
+        first = 0
+        for block in BLOCKS:
+            for c in range(first, first + len(block)):
+                for tile in range(GROUP_UNITS):
+                    unit = GROUP_UNITS * c + tile
+                    late = tile * len(block) if first + len(block) < GROUPS else 0
+                    steps = [order.index(PASSES * c + g) + late for g in range(PASSES)]
+                    for g in range(PASSES):
+                        passes_at.setdefault(steps[g], []).append((unit, g))
+                    finished_at.setdefault(steps[PASSES - 1], []).append(unit)
+                    starts.append((steps[0], unit))
+            first += len(block)
+        bank_of = {unit: turn % BANKS for turn, (start, unit) in enumerate(sorted(starts))}
+
         loads = []
         for i, heads in enumerate(LOAD_HEADS):
             loads.extend((g, sum(LOAD_HEADS[:i]), heads) for g in range(PASSES))
@@ -193,6 +214,9 @@ def tile_multiheadattention_pa_kernel(tc, x, w, out):
         for i in range(GROUP_UNITS):
             for half in range(2):
                 turn_x(i, half)
+        warm = bank(0, [P, WARM_COLS], "warm")
+        for i in range(WARM_MATMULS):
+            nc.tensor.matmul(warm[:], lhsT=x_bf16[0][:, :P], rhs=x_bf16[0][:, :WARM_COLS], start=True, stop=True)
         regroup_w(0)
         regroup_w(1)
         quantise_w(0)
@@ -220,17 +244,15 @@ def tile_multiheadattention_pa_kernel(tc, x, w, out):
                 quantise_w(j + 2)
             for pair in finish:
                 invert(pair)
-            c, g = divmod(order[j], PASSES) if j < chunks else (0, -1)
-            units = range(GROUP_UNITS * c, GROUP_UNITS * (c + 1)) if j < chunks else ()
-            for unit in units:
+            for unit, g in passes_at.get(j, []):
                 multiply(unit, g)
-            if j > 1:
-                regroup_w(j + 3)
             summed = to_sum[: GROUP_UNITS if j >= chunks - 1 else 1]
             for unit in summed:
                 sum_heads(unit)
                 if unit % TOKEN_TILES == TOKEN_TILES - 1:
-                    to_finish.append((j + (2 if j < chunks - 1 else 1), unit // TOKEN_TILES))
-            to_sum = to_sum[len(summed) :] + (list(units) if g == PASSES - 1 else [])
+                    to_finish.append((j + 1, unit // TOKEN_TILES))
+            to_sum = to_sum[len(summed) :] + finished_at.get(j, [])
+            if j > 1:
+                regroup_w(j + 3)
             for pair in finish:
                 scale_and_store(pair)

@@ -28,7 +28,7 @@ WORDS = K_PASS // 2
 WARM_MATMULS = 5
 WARM_COLS = 512
 EARLY_STEPS = 8
-EARLY_SHARE = 18
+EARLY_SHARE = 16
 VECTOR_SHARE = 20
 
 FLOPS = 2 * B * S * D * H * DH
@@ -224,13 +224,16 @@ def tile_multiheadattention_pa_kernel(tc, x, w, out):
         for i in range(GROUP_UNITS):
             for half in range(2):
                 empty_x(i, half)
-            if i % 2 == 1:
-                quantise_x(i - 1)
-                regroup_w(2 + i // 2)
-                quantise_x(i)
             if i == 1:
+                quantise_x(0)
+                regroup_w(2)
+                quantise_x(1)
+                regroup_w(3)
                 quantise_w(2)
-        regroup_w(4)
+            if i == 3:
+                quantise_x(2)
+                regroup_w(4)
+                quantise_x(3)
 
         to_sum = []
         to_finish = []

@@ -17,18 +17,18 @@ B, S, D, H, DH = 2, 256, 2048, 16, 128
 EPS = 1e-6
 PASSES = D // K_PASS
 TOKEN_TILES = S // P
-BLOCKS = ((4, 2), (4, 2), (2,), (1,), (1,))
+BLOCKS = ((4, 4), (4,), (2,), (1,), (1,))
 GROUP_HEADS = sum(BLOCKS, ())
 GROUPS = len(GROUP_HEADS)
 FIRST_HEAD = [sum(GROUP_HEADS[:c]) for c in range(GROUPS)]
-LOAD_HEADS = (6, 6, 4)
+LOAD_HEADS = (8, 4, 4)
 GROUP_UNITS = B * TOKEN_TILES
 BANKS = 8
 WORDS = K_PASS // 2
-WARM_MATMULS = 5
+WARM_MATMULS = 3
 WARM_COLS = 512
 EARLY_STEPS = 8
-EARLY_SHARE = 16
+EARLY_SHARE = 18
 VECTOR_SHARE = 20
 
 FLOPS = 2 * B * S * D * H * DH
@@ -190,7 +190,7 @@ def tile_multiheadattention_pa_kernel(tc, x, w, out):
             for c in range(first, first + len(block)):
                 for tile in range(GROUP_UNITS):
                     unit = GROUP_UNITS * c + tile
-                    late = tile * len(block) if first + len(block) < GROUPS else 0
+                    late = tile if first + len(block) < GROUPS else 0
                     steps = [order.index(PASSES * c + g) + late for g in range(PASSES)]
                     for g in range(PASSES):
                         passes_at.setdefault(steps[g], []).append((unit, g))
@@ -230,10 +230,9 @@ def tile_multiheadattention_pa_kernel(tc, x, w, out):
                 quantise_x(1)
                 regroup_w(3)
                 quantise_w(2)
-            if i == 3:
-                quantise_x(2)
-                regroup_w(4)
-                quantise_x(3)
+            if i > 1:
+                quantise_x(i)
+        regroup_w(4)
 
         to_sum = []
         to_finish = []
@@ -249,7 +248,7 @@ def tile_multiheadattention_pa_kernel(tc, x, w, out):
                 invert(pair)
             for unit, g in passes_at.get(j, []):
                 multiply(unit, g)
-            summed = to_sum[: GROUP_UNITS if j >= chunks - 1 else 1]
+            summed = to_sum[: GROUP_UNITS if j >= chunks - 1 else 2 if j <= EARLY_STEPS else 1]
             for unit in summed:
                 sum_heads(unit)
                 if unit % TOKEN_TILES == TOKEN_TILES - 1:

from contextlib import ExitStack

import concourse.mybir as mybir
from concourse.masks import make_identity

F32 = mybir.dt.float32
BF16 = mybir.dt.bfloat16
U32 = mybir.dt.uint32
U8 = mybir.dt.uint8
FP8X4 = mybir.dt.float8_e4m3fn_x4
COPY = mybir.ActivationFunctionType.Copy

P = 128
PACK = 4
K_PASS = P * PACK
B, S, D, H, DH = 2, 256, 2048, 16, 128
EPS = 1e-6
PASSES = D // K_PASS
TOKEN_TILES = S // P
BLOCKS = ((4, 4), (4,), (2,), (1,), (1,))
GROUP_HEADS = sum(BLOCKS, ())
GROUPS = len(GROUP_HEADS)
FIRST_HEAD = [sum(GROUP_HEADS[:c]) for c in range(GROUPS)]
LOAD_HEADS = (8, 4, 4)
GROUP_UNITS = B * TOKEN_TILES
BANKS = 8
WORDS = K_PASS // 2
WARM_MATMULS = 3
WARM_COLS = 512
EARLY_STEPS = 8
EARLY_SHARE = 18
VECTOR_SHARE = 20

FLOPS = 2 * B * S * D * H * DH


def tile_multiheadattention_pa_kernel(tc, x, w, out):
    nc = tc.nc
    with ExitStack() as ctx:
        keep = ctx.enter_context(tc.tile_pool(name="keep", bufs=1))
        stage = ctx.enter_context(tc.tile_pool(name="stage", bufs=5))
        results = ctx.enter_context(tc.tile_pool(name="results", bufs=B * GROUPS))
        psum = ctx.enter_context(tc.psum_pool(name="psum", bufs=1))
        ctx.enter_context(tc.manual_schedule())

        ident = keep.tile([P, P], F32)
        make_identity(nc, ident[:])

        x_raw = {}
        x_bf16 = {}
        x_grouped = keep.tile([P, GROUP_UNITS * PASSES * P * PACK], BF16, align_bytes=64)
        x_grouped_cols = x_grouped[:].rearrange("p (i c) -> p i c", i=GROUP_UNITS)
        x_grouped_words = x_grouped[:].bitcast(F32).rearrange("p (i g r u) -> p i g r u", i=GROUP_UNITS, g=PASSES, u=2)
        x_codes = keep.tile([P, GROUP_UNITS, PASSES * P], U32, align_bytes=64)
        x_scales = keep.tile([P, GROUP_UNITS, PASSES * P], U8, align_bytes=64)

        chunks = GROUPS * PASSES
        order = []
        for block in BLOCKS:
            first = len(order) // PASSES
            order.extend(PASSES * c + g for g in range(PASSES) for c in range(first, first + len(block)))
        w_raw = {}
        w_codes = keep.tile([P, PASSES, H * DH], U32, align_bytes=64)
        w_scales = keep.tile([P, PASSES, H * DH], U8, align_bytes=64)

        def chunk_cols(j):
            c = j // PASSES
            return slice(DH * FIRST_HEAD[c], DH * (FIRST_HEAD[c] + GROUP_HEADS[c]))

        def bank(index, shape, name):
            return psum.tile(shape, F32, tag="bank%d" % index, name=name)

        def load_w(g, h0, heads):
            raw = keep.tile([P, PACK, heads * DH], BF16, name="raw_%d_%d" % (g, h0))
            rows = w[K_PASS * g : K_PASS * (g + 1), DH * h0 : DH * (h0 + heads)]
            nc.sync.dma_start(out=raw[:], in_=rows.rearrange("(p t) n -> p t n", t=PACK))
            for c in range(GROUPS):
                if h0 <= FIRST_HEAD[c] < h0 + heads:
                    n0 = DH * (FIRST_HEAD[c] - h0)
                    w_raw[PASSES * c + g] = raw[:, :, n0 : n0 + DH * GROUP_HEADS[c]]

        def load_x(i):
            b, m = divmod(i, TOKEN_TILES)
            raw = keep.tile([P, D], BF16, name="x_%d" % i)
            nc.sync.dma_start(out=raw[:], in_=x[b].rearrange("(p m) k -> p m k", m=TOKEN_TILES)[:, m, :])
            x_bf16[i] = raw
            x_raw[i] = raw[:].bitcast(F32)

        xt = {}

        def turn_x(i, half):
            xt[(i, half)] = bank(TOKEN_TILES * i + half, [P, 2, 2, P], "xt")
            for part in range(2):
                for u in range(2):
                    g = 2 * half + part
                    nc.tensor.transpose(xt[(i, half)][:, part, u, :], x_raw[i][:, WORDS * g + u : WORDS * (g + 1) : 2], ident[:])

        def empty_x(i, half):
            nc.scalar.copy(
                out=x_grouped_words[:, i, 2 * half : 2 * half + 2], in_=xt[(i, half)][:].rearrange("p g u r -> p g r u")
            )

        def quantise_x(i):
            nc.vector.quantize_mx(out=x_codes[:, i, :].bitcast(FP8X4), scales=x_scales[:, i, :], in_=x_grouped_cols[:, i, :])

        grouped = {}

        def regroup_w(step):
            if step >= chunks:
                return
            j = order[step]
            cols = DH * GROUP_HEADS[j // PASSES]
            grouped[j] = stage.tile([P, cols, PACK], BF16, align_bytes=64, tag="grouped", name="grouped")
            dst = grouped[j][:].rearrange("p (c i) t -> p c t i", i=4)
            src = w_raw[j].rearrange("p t (c i) -> p c t i", i=4)
            split = cols // 32 * (EARLY_SHARE if step < EARLY_STEPS else VECTOR_SHARE) // 8 * 2
            nc.vector.tensor_copy(out=dst[:, :split], in_=src[:, :split])
            nc.scalar.copy(out=dst[:, split:], in_=src[:, split:])

        def quantise_w(step):
            j = order[step]
            nc.vector.quantize_mx(
                out=w_codes[:, j % PASSES, chunk_cols(j)].bitcast(FP8X4),
                scales=w_scales[:, j % PASSES, chunk_cols(j)],
                in_=grouped[j][:].rearrange("p n t -> p (n t)"),
            )

        acc = {}

        def multiply(unit, g):
            c, tile = divmod(unit, GROUP_UNITS)
            if g == 0:
                acc[unit] = bank(bank_of[unit], [P, DH * GROUP_HEADS[c]], "acc")
            tokens = slice(P * g, P * (g + 1))
            nc.tensor.matmul_mx(
                out=acc[unit][:],
                lhsT=x_codes[:, tile, tokens].bitcast(FP8X4),
                lhsT_scale=x_scales[:, tile, tokens],
                rhs=w_codes[:, g, chunk_cols(PASSES * c)].bitcast(FP8X4),
                rhs_scale=w_scales[:, g, chunk_cols(PASSES * c)],
                start=(g == 0),
                stop=(g == PASSES - 1),
            )

        y = {}
        sums = {}
        inverse = {}

        def sum_heads(unit):
            pair, m = divmod(unit, TOKEN_TILES)
            heads = GROUP_HEADS[pair // B]
            if m == 0:
                y[pair] = results.tile([P, heads, TOKEN_TILES, DH], F32, tag="y", name="y")
                sums[pair] = results.tile([P, TOKEN_TILES, heads], F32, tag="sums", name="sums")
                inverse[pair] = results.tile([P, TOKEN_TILES, heads], F32, tag="inverse", name="inverse")
            for h in range(heads):
                nc.scalar.activation(
                    out=y[pair][:, h, m, :],
                    in_=acc[unit][:, DH * h : DH * (h + 1)],
                    func=COPY,
                    accum_out=sums[pair][:, m, h : h + 1],
                )

        def add_eps(pair):
            nc.vector.tensor_scalar_add(out=inverse[pair][:], in0=sums[pair][:], scalar1=EPS)

        def invert(pair):
            nc.vector.reciprocal(out=inverse[pair][:], in_=inverse[pair][:])

        def scale_and_store(pair):
            c, b = divmod(pair, B)
            for m in range(TOKEN_TILES):
                for h in range(GROUP_HEADS[c]):
                    nc.vector.tensor_scalar_mul(
                        out=y[pair][:, h, m, :], in0=y[pair][:, h, m, :], scalar1=inverse[pair][:, m, h : h + 1]
                    )
            nc.sync.dma_start(
                out=out[b, FIRST_HEAD[c] : FIRST_HEAD[c] + GROUP_HEADS[c]].rearrange(
                    "h (p m) d -> p h (m d)", m=TOKEN_TILES
                ),
                in_=y[pair][:].rearrange("p h m d -> p h (m d)"),
            )


        passes_at = {}
        finished_at = {}
        starts = []
        first = 0
        for block in BLOCKS:
            for c in range(first, first + len(block)):
                for tile in range(GROUP_UNITS):
                    unit = GROUP_UNITS * c + tile
                    late = tile if first + len(block) < GROUPS else 0
                    steps = [order.index(PASSES * c + g) + late for g in range(PASSES)]
                    for g in range(PASSES):
                        passes_at.setdefault(steps[g], []).append((unit, g))
                    finished_at.setdefault(steps[PASSES - 1], []).append(unit)
                    starts.append((steps[0], unit))
            first += len(block)
        bank_of = {unit: turn % BANKS for turn, (start, unit) in enumerate(sorted(starts))}

        loads = []
        for i, heads in enumerate(LOAD_HEADS):
            loads.extend((g, sum(LOAD_HEADS[:i]), heads) for g in range(PASSES))
        load_w(*loads[0])
        load_x(0)
        load_x(1)
        load_w(*loads[1])
        load_x(2)
        load_x(3)
        for g, h0, heads in loads[2:]:
            load_w(g, h0, heads)

        for i in range(GROUP_UNITS):
            for half in range(2):
                turn_x(i, half)
        warm = bank(0, [P, WARM_COLS], "warm")
        for i in range(WARM_MATMULS):
            nc.tensor.matmul(warm[:], lhsT=x_bf16[0][:, :P], rhs=x_bf16[0][:, :WARM_COLS], start=True, stop=True)
        regroup_w(0)
        regroup_w(1)
        quantise_w(0)
        quantise_w(1)
        for i in range(GROUP_UNITS):
            for half in range(2):
                empty_x(i, half)
            if i == 1:
                quantise_x(0)
                regroup_w(2)
                quantise_x(1)
                regroup_w(3)
                quantise_w(2)
            if i > 1:
                quantise_x(i)
        regroup_w(4)

        to_sum = []
        to_finish = []
        for j in range(chunks + 6):
            finish = [pair for step, pair in to_finish if step == j]
            for pair in finish:
                add_eps(pair)
            if 1 < j < chunks - 2:
                quantise_w(j + 1)
            if j == chunks - 3:
                quantise_w(j + 2)
            for pair in finish:
                invert(pair)
            for unit, g in passes_at.get(j, []):
                multiply(unit, g)
            summed = to_sum[: GROUP_UNITS if j >= chunks - 1 else 2 if j <= EARLY_STEPS else 1]
            for unit in summed:
                sum_heads(unit)
                if unit % TOKEN_TILES == TOKEN_TILES - 1:
                    to_finish.append((j + 1, unit // TOKEN_TILES))
            to_sum = to_sum[len(summed) :] + finished_at.get(j, [])
            if j > 1:
                regroup_w(j + 3)
            for pair in finish:
                scale_and_store(pair)
